import numpy as np
import ml_dtypes


def mxq(x, axis, fmt="e4m3"):
    dtype, down = {"e4m3": (ml_dtypes.float8_e4m3fn, 7), "e5m2": (ml_dtypes.float8_e5m2, 14)}[fmt]
    v = np.moveaxis(np.asarray(x, np.float32).astype(ml_dtypes.bfloat16).astype(np.float64), axis, -1)
    blocks = v.reshape(v.shape[:-1] + (-1, 32))
    amax = np.abs(blocks).max(-1, keepdims=True)
    byte = np.maximum(np.where(amax > 0, np.frexp(amax)[1] - 1 + 127, 0) - down, 1)
    scale = np.exp2(byte - 127.0)
    codes = (blocks / scale).astype(np.float32).astype(dtype).astype(np.float64)
    return np.moveaxis((codes * scale).reshape(v.shape), -1, axis)


WIDE = False


def mx_kscale(k):
    if not WIDE:
        return np.ones(k)
    levels = np.array([10, -10, 5, -5, 0])
    a = np.random.permutation(np.resize(levels, k // 512 * 4)).reshape(k // 512, 4)
    idx = np.arange(k)
    return np.exp2(a[idx // 512, idx % 128 // 32])


BF16 = ml_dtypes.bfloat16


def bf(x):
    return np.asarray(x, np.float32).astype(BF16)


def f64(x):
    return np.asarray(x).astype(np.float64)


N, C, S, H = 8192, 1024, 128, 4
DH = C // H


def setup_inputs():
    t = mx_kscale(C)
    return {"qp": bf(np.random.standard_normal((S, C)) * 1.5 / np.sqrt(DH)),
            "kp": bf(np.random.standard_normal((N, C)) * 1.5),
            "vp": bf(np.random.standard_normal((N, C)) * 3.0 * t[None, :]),
            "out_proj_w": bf(np.random.standard_normal((C, C)) * 5.0 / np.sqrt(C) / t[None, :]),
            "out_proj_b": bf(0.1 * np.random.standard_normal(C))}


def reference(qp, kp, vp, out_proj_w, out_proj_b):
    q = f64(qp).reshape(S, H, DH).transpose(1, 0, 2)
    k = f64(kp).reshape(N, H, DH).transpose(1, 2, 0)
    v = f64(vp).reshape(N, H, DH).transpose(1, 0, 2)
    s = q @ k
    e = np.exp(s - s.max(-1, keepdims=True))
    o = (mxq(e, 2, "e4m3") @ mxq(v, 1, "e4m3")) / e.sum(-1, keepdims=True)
    o = o.transpose(1, 0, 2).reshape(S, C)
    y = (mxq(o, 1, "e4m3") @ mxq(f64(out_proj_w), 1, "e4m3").T) + f64(out_proj_b)
    return y.mean(axis=0)

@@ -1,0 +1,313 @@
+from contextlib import ExitStack
+
+import concourse.mybir as mybir
+from concourse.masks import make_identity
+
+F32 = mybir.dt.float32
+BF16 = mybir.dt.bfloat16
+U8 = mybir.dt.uint8
+U32 = mybir.dt.uint32
+FP8X4 = mybir.dt.float8_e4m3fn_x4
+ALU = mybir.AluOpType
+ACT = mybir.ActivationFunctionType
+AX = mybir.AxisListType
+
+P = 128
+H = 4
+NCH = 16
+NV = 8
+
+FLOPS = 2 * 128 * 8192 * 1024 * 2 + 2 * 128 * 1024 * 1024
+
+
+def copy_on(nc, eng, out, in_):
+    if eng == "v":
+        nc.vector.tensor_copy(out=out, in_=in_)
+    elif eng == "s":
+        nc.scalar.copy(out=out, in_=in_)
+    else:
+        nc.gpsimd.tensor_scalar(out=out, in0=in_, scalar1=1.0, scalar2=0.0, op0=ALU.mult, op1=ALU.add)
+
+
+def tile_pma_pb_t_kernel(tc, qp, kp, vp, out_proj_w, out_proj_b, out):
+    nc = tc.nc
+    with ExitStack() as ctx:
+        const = ctx.enter_context(tc.tile_pool(name="const", bufs=1))
+        s_pool = ctx.enter_context(tc.tile_pool(name="s_pool", bufs=32))
+        kraw_pool = ctx.enter_context(tc.tile_pool(name="kraw_pool", bufs=2))
+        vraw_pool = ctx.enter_context(tc.tile_pool(name="vraw_pool", bufs=2))
+        kt_pool = ctx.enter_context(tc.tile_pool(name="kt_pool", bufs=2))
+        vgrp_pool = ctx.enter_context(tc.tile_pool(name="vgrp_pool", bufs=2))
+        vc_pool = ctx.enter_context(tc.tile_pool(name="vc_pool", bufs=NV))
+        psum = ctx.enter_context(tc.psum_pool(name="psum", bufs=4))
+
+        ident_f = const.tile([P, P], F32, name="ident_f")
+        make_identity(nc, ident_f[:])
+        ident_b = const.tile([P, P], BF16, name="ident_b")
+        make_identity(nc, ident_b[:])
+        warm = const.tile([P, 1], F32, name="warm")
+        nc.vector.memset(warm[:], 0.0)
+        warm2 = const.tile([P, 1], F32, name="warm2")
+        nc.scalar.activation(out=warm2[:], in_=warm[:], func=ACT.Exp)
+
+        mx = const.tile([P, H * NCH], F32, name="mx")
+        negm = const.tile([P, H], F32, name="negm")
+        rs = const.tile([P, H * 8], F32, name="rs")
+        rsum = const.tile([P, H], F32, name="rsum")
+        rinv = const.tile([P, H], F32, name="rinv")
+        b_raw = const.tile([P, 8], BF16, name="b_raw")
+        b32 = const.tile([P, 8], F32, name="b32")
+        ysum = const.tile([P, 8], F32, name="ysum")
+        res = const.tile([P, 8], F32, name="res")
+
+        q_sb = const.tile([P, 1024], BF16, name="q_sb")
+        nc.sync.dma_start(out=q_sb[:], in_=qp)
+        nc.scalar.dma_start(out=b_raw[:], in_=out_proj_b.rearrange("(p i) -> p i", i=8))
+        nc.vector.tensor_copy(out=b32[:], in_=b_raw[:])
+
+        kraws = {}
+        vraws = {}
+        kts = {}
+        vcs = {}
+        vss = {}
+        s_tiles = {}
+
+        def k_load(c):
+            t = kraw_pool.tile([P, 4096], BF16, name="kraw", tag="kraw")
+            nc.sync.dma_start(out=t[:], in_=kp[512 * c:512 * c + 512, :].rearrange("(p j) f -> p (j f)", j=4))
+            kraws[c] = t
+
+        def v_load(i):
+            t = vraw_pool.tile([P, 4096], BF16, name="vraw", tag="vraw")
+            nc.sync.dma_start(out=t[:], in_=vp[512 * i:512 * i + 512, :].rearrange("(p j) f -> p (j f)", j=4))
+            vraws[i] = t
+
+        k_load(0)
+        k_load(1)
+
+        qt_ps = psum.tile([P, 512], F32, name="qt_ps", tag="pa")
+        for h in range(H):
+            nc.tensor.transpose(qt_ps[:, 128 * h:128 * h + 128], q_sb[:].bitcast(F32)[:, 128 * h:128 * h + 128], ident_f[:])
+        qT = const.tile([P, 1024], BF16, name="qT")
+        nc.vector.tensor_copy(
+            out=qT[:].rearrange("p (e n) -> p e n", e=2),
+            in_=qt_ps[:].bitcast(BF16).rearrange("p (n e) -> p e n", e=2),
+        )
+
+        def k_transpose(c):
+            kt = kt_pool.tile([P, 4096], BF16, name="kt", tag="kt")
+            kw = kraws[c][:].bitcast(F32)
+            for h in range(H):
+                kt_ps = psum.tile([P, 512], F32, name="kt_ps", tag="pa")
+                for j in range(4):
+                    nc.tensor.transpose(kt_ps[:, 128 * j:128 * j + 128], kw[:, 512 * j + 128 * h:512 * j + 128 * h + 128], ident_f[:])
+                nc.scalar.copy(out=kt[:].bitcast(F32)[:, 512 * h:512 * h + 512], in_=kt_ps[:])
+            kts[c] = kt
+
+        def k_scores(c):
+            kv = kts[c][:].rearrange("p (n e) -> p n e", e=2)
+            for h in range(H):
+                if c % 2 == 0:
+                    s_tiles[(h, c // 2)] = s_pool.tile([P, 1024], F32, name="s_t", tag="s", align_bytes=64)
+                s_ps = psum.tile([P, 512], F32, name="s_ps", tag="pb")
+                for e in range(2):
+                    nc.tensor.matmul(
+                        out=s_ps[:],
+                        lhsT=qT[:, 512 * e + 128 * h:512 * e + 128 * h + 128],
+                        rhs=kv[:, 512 * h:512 * h + 512, e],
+                        start=(e == 0),
+                        stop=(e == 1),
+                    )
+                nc.vector.tensor_scalar(
+                    out=s_tiles[(h, c // 2)][:, 512 * (c % 2):512 * (c % 2) + 512],
+                    in0=s_ps[:],
+                    scalar1=1.0,
+                    scalar2=None,
+                    op0=ALU.mult,
+                    op1=ALU.max,
+                    accum_out=mx[:, NCH * h + c:NCH * h + c + 1],
+                )
+
+        def v_prep(i, engines):
+            vc = vc_pool.tile([P, 1024], U32, name="vc", tag="vc", align_bytes=64)
+            vs = vc_pool.tile([P, 1024], U8, name="vs", tag="vs", align_bytes=64)
+            groups = []
+            for u in range(2):
+                g = vgrp_pool.tile([P, 2048], BF16, name="vgrp", tag="vgrp", align_bytes=64)
+                dst = g[:].rearrange("p (c i t) -> p c t i", i=4, t=4)
+                src = vraws[i][:].rearrange("p (t f) -> p t f", t=4)[:, :, 512 * u:512 * u + 512].rearrange(
+                    "p t (c i) -> p c t i", i=4
+                )
+                copy_on(nc, engines[u], dst, src)
+                groups.append(g)
+            for u in range(2):
+                nc.vector.quantize_mx(
+                    out=vc[:, 512 * u:512 * u + 512].bitcast(FP8X4),
+                    scales=vs[:, 512 * u:512 * u + 512],
+                    in_=groups[u][:],
+                )
+            vcs[i] = vc
+            vss[i] = vs
+
+        k_transpose(0)
+        for c in range(NCH):
+            if c + 2 < NCH:
+                k_load(c + 2)
+            if c % 2 == 0:
+                v_load(c // 2)
+            if c + 1 < NCH:
+                k_transpose(c + 1)
+            k_scores(c)
+            if c % 2 == 1:
+                v_prep(c // 2, ("s", "v"))
+
+        v_load(8)
+        v_load(9)
+        wraws = []
+        w_view = out_proj_w.rearrange("(p i) k -> p i k", i=8)
+        for ih in range(2):
+            t = kraw_pool.tile([P, 4096], BF16, name="wraw", tag="kraw")
+            nc.sync.dma_start(out=t[:].rearrange("p (i k) -> p i k", i=4), in_=w_view[:, 4 * ih:4 * ih + 4, :])
+            wraws.append(t)
+
+        nc.vector.tensor_reduce(
+            out=negm[:], in_=mx[:].rearrange("p (h c) -> p h c", h=H), axis=AX.X, op=ALU.max, negate=True
+        )
+
+        o_ps = []
+        for h in range(H):
+            o_ps.append(psum.tile([P, 512], F32, name="o_ps", tag="pb"))
+
+        wcs = []
+        wss = []
+
+        def w_prep(g):
+            wc = vc_pool.tile([P, 1024], U32, name="wc", tag="vc", align_bytes=64)
+            ws = vc_pool.tile([P, 1024], U8, name="ws", tag="vs", align_bytes=64)
+            for ih in range(2):
+                ww = wraws[ih][:].bitcast(F32)
+                wg = vgrp_pool.tile([P, 2048], BF16, name="wgrp", tag="vgrp", align_bytes=64)
+                for ip in range(2):
+                    wt_ps = psum.tile([P, 512], F32, name="wt_ps", tag="pa")
+                    for i2 in range(2):
+                        il = 2 * ip + i2
+                        for u in range(2):
+                            col = 512 * il + 256 * g + 128 * u
+                            nc.tensor.transpose(
+                                wt_ps[:, 256 * i2 + 128 * u:256 * i2 + 128 * u + 128], ww[:, col:col + 128], ident_f[:]
+                            )
+                    copy_on(
+                        nc,
+                        "s" if ip == 0 else "v",
+                        wg[:].bitcast(F32)[:, 512 * ip:512 * ip + 512].rearrange("q (i p u) -> q i p u", i=2, u=2),
+                        wt_ps[:].rearrange("q (i u p) -> q i p u", i=2, u=2),
+                    )
+                nc.vector.quantize_mx(
+                    out=wc[:, 512 * ih:512 * ih + 512].bitcast(FP8X4),
+                    scales=ws[:, 512 * ih:512 * ih + 512],
+                    in_=wg[:],
+                )
+            wcs.append(wc)
+            wss.append(ws)
+
+        for cc in range(8):
+            e_sb = kt_pool.tile([P, 4096], BF16, name="e_sb", tag="kt")
+            for h in range(H):
+                nc.scalar.activation(
+                    out=e_sb[:, 1024 * h:1024 * h + 1024],
+                    in_=s_tiles[(h, cc)][:],
+                    func=ACT.Exp,
+                    bias=negm[:, h:h + 1],
+                    scale=1.0,
+                    accum_out=rs[:, 8 * h + cc:8 * h + cc + 1],
+                )
+            ec2 = s_pool.tile([P, 1024], U32, name="ec2", tag="s", align_bytes=64)
+            es2 = s_pool.tile([P, 1024], U8, name="es2", tag="s", align_bytes=64)
+            for half in range(2):
+                c = 2 * cc + half
+                egrp = s_pool.tile([P, 2048], BF16, name="egrp", tag="s", align_bytes=64)
+                for hp in range(2):
+                    et_ps = psum.tile([P, 1024], BF16, name="et_ps", tag="pa")
+                    for hh in range(2):
+                        h = 2 * hp + hh
+                        for t in range(4):
+                            col = 1024 * h + 512 * half + 128 * t
+                            nc.tensor.transpose(
+                                et_ps[:, 512 * hh + 128 * t:512 * hh + 128 * t + 128], e_sb[:, col:col + 128], ident_b[:]
+                            )
+                    copy_on(
+                        nc,
+                        "s" if hp == 0 else "v",
+                        egrp[:, 1024 * hp:1024 * hp + 1024].rearrange("p (h s t) -> p h s t", h=2, t=4),
+                        et_ps[:].rearrange("p (h t s) -> p h s t", h=2, t=4),
+                    )
+                nc.vector.quantize_mx(
+                    out=ec2[:, 512 * half:512 * half + 512].bitcast(FP8X4),
+                    scales=es2[:, 512 * half:512 * half + 512],
+                    in_=egrp[:],
+                )
+                for h in range(H):
+                    ecol = 512 * half + 128 * h
+                    nc.tensor.matmul_mx(
+                        out=o_ps[h][:, 0:256],
+                        lhsT=ec2[:, ecol:ecol + 128].bitcast(FP8X4),
+                        lhsT_scale=es2[:, ecol:ecol + 128],
+                        rhs=vcs[c][:, 256 * h:256 * h + 256].bitcast(FP8X4),
+                        rhs_scale=vss[c][:, 256 * h:256 * h + 256],
+                        start=(c == 0),
+                        stop=(c == NCH - 1),
+                    )
+                if half == 0:
+                    v_prep(8 + cc, ("v", "v"))
+                    if 8 + cc + 2 < NCH:
+                        v_load(8 + cc + 2)
+            if cc == 5:
+                w_prep(0)
+            if cc == 6:
+                w_prep(1)
+
+        nc.vector.tensor_reduce(out=rsum[:], in_=rs[:].rearrange("p (h c) -> p h c", h=H), axis=AX.X, op=ALU.add)
+        nc.vector.reciprocal(out=rinv[:], in_=rsum[:])
+        o_sb = const.tile([P, 1024], BF16, name="o_sb")
+        for h in range(H):
+            dst = o_sb[:, 256 * h:256 * h + 256].rearrange("s (e p) -> s e p", e=2)
+            src = o_ps[h][:, 0:256].rearrange("s (p e) -> s e p", e=2)
+            if h % 2 == 0:
+                nc.vector.tensor_scalar(out=dst, in0=src, scalar1=rinv[:, h:h + 1], scalar2=None, op0=ALU.mult)
+            else:
+                nc.scalar.activation(out=dst, in_=src, func=ACT.Copy, scale=rinv[:, h:h + 1])
+        ot_ps = psum.tile([P, 1024], BF16, name="ot_ps", tag="pa")
+        for b8 in range(8):
+            nc.tensor.transpose(ot_ps[:, 128 * b8:128 * b8 + 128], o_sb[:, 128 * b8:128 * b8 + 128], ident_b[:])
+        ogrp = const.tile([P, 1024], BF16, name="ogrp", align_bytes=64)
+        for g in range(2):
+            copy_on(
+                nc,
+                "s" if g == 0 else "v",
+                ogrp[:, 512 * g:512 * g + 512].rearrange("p (s t) -> p s t", t=4),
+                ot_ps[:, 512 * g:512 * g + 512].rearrange("p (t s) -> p s t", t=4),
+            )
+        oc = const.tile([P, 256], U32, name="oc", align_bytes=64)
+        osc = const.tile([P, 256], U8, name="osc", align_bytes=64)
+        nc.vector.quantize_mx(out=oc[:].bitcast(FP8X4), scales=osc[:], in_=ogrp[:])
+        for b in range(2):
+            y_ps = psum.tile([P, 512], F32, name="y_ps", tag="pa")
+            for i4 in range(4):
+                i = 4 * b + i4
+                for g in range(2):
+                    nc.tensor.matmul_mx(
+                        out=y_ps[:, 128 * i4:128 * i4 + 128],
+                        lhsT=wcs[g][:, 128 * i:128 * i + 128].bitcast(FP8X4),
+                        lhsT_scale=wss[g][:, 128 * i:128 * i + 128],
+                        rhs=oc[:, 128 * g:128 * g + 128].bitcast(FP8X4),
+                        rhs_scale=osc[:, 128 * g:128 * g + 128],
+                        start=(g == 0),
+                        stop=(g == 1),
+                    )
+            nc.vector.tensor_reduce(
+                out=ysum[:, 4 * b:4 * b + 4], in_=y_ps[:].rearrange("p (i s) -> p i s", i=4), axis=AX.X, op=ALU.add
+            )
+        nc.vector.scalar_tensor_tensor(
+            out=res[:], in0=ysum[:], scalar=1.0 / 128.0, in1=b32[:], op0=ALU.mult, op1=ALU.add
+        )
+        nc.sync.dma_start(out=out.rearrange("(p i) -> p i", i=8), in_=res[:])

@@ -16,6 +16,11 @@ P = 128
 H = 4
 NCH = 16
 NV = 8
+KB = 3
+V_LAG = 1
+FILL_STEPS = 1
+DOUBLE = (1, 2)
+W_FIRST = 3
 
 FLOPS = 2 * 128 * 8192 * 1024 * 2 + 2 * 128 * 1024 * 1024
 
@@ -34,12 +39,19 @@ def tile_pma_pb_t_kernel(tc, qp, kp, vp, out_proj_w, out_proj_b, out):
     with ExitStack() as ctx:
         const = ctx.enter_context(tc.tile_pool(name="const", bufs=1))
         s_pool = ctx.enter_context(tc.tile_pool(name="s_pool", bufs=32))
-        kraw_pool = ctx.enter_context(tc.tile_pool(name="kraw_pool", bufs=2))
+        kraw_pool = ctx.enter_context(tc.tile_pool(name="kraw_pool", bufs=KB))
         vraw_pool = ctx.enter_context(tc.tile_pool(name="vraw_pool", bufs=2))
         kt_pool = ctx.enter_context(tc.tile_pool(name="kt_pool", bufs=2))
         vgrp_pool = ctx.enter_context(tc.tile_pool(name="vgrp_pool", bufs=2))
         vc_pool = ctx.enter_context(tc.tile_pool(name="vc_pool", bufs=NV))
         psum = ctx.enter_context(tc.psum_pool(name="psum", bufs=4))
+        ctx.enter_context(tc.manual_schedule())
+
+        def bank_a(shape, dtype, name):
+            return psum.tile(shape, dtype, name=name, tag="pa", bufs=3)
+
+        def bank_w(shape, dtype, name):
+            return psum.tile(shape, dtype, name=name, tag="pw", bufs=1)
 
         ident_f = const.tile([P, P], F32, name="ident_f")
         make_identity(nc, ident_f[:])
@@ -60,17 +72,15 @@ def tile_pma_pb_t_kernel(tc, qp, kp, vp, out_proj_w, out_proj_b, out):
         ysum = const.tile([P, 8], F32, name="ysum")
         res = const.tile([P, 8], F32, name="res")
 
-        q_sb = const.tile([P, 1024], BF16, name="q_sb")
-        nc.sync.dma_start(out=q_sb[:], in_=qp)
-        nc.scalar.dma_start(out=b_raw[:], in_=out_proj_b.rearrange("(p i) -> p i", i=8))
-        nc.vector.tensor_copy(out=b32[:], in_=b_raw[:])
-
         kraws = {}
         vraws = {}
         kts = {}
         vcs = {}
         vss = {}
+        grps = {}
         s_tiles = {}
+        wraws = []
+        w_view = out_proj_w.rearrange("(p i) k -> p i k", i=8)
 
         def k_load(c):
             t = kraw_pool.tile([P, 4096], BF16, name="kraw", tag="kraw")
@@ -79,34 +89,46 @@ def tile_pma_pb_t_kernel(tc, qp, kp, vp, out_proj_w, out_proj_b, out):
 
         def v_load(i):
             t = vraw_pool.tile([P, 4096], BF16, name="vraw", tag="vraw")
-            nc.sync.dma_start(out=t[:], in_=vp[512 * i:512 * i + 512, :].rearrange("(p j) f -> p (j f)", j=4))
+            (nc.sync if i < 2 else nc.gpsimd).dma_start(out=t[:], in_=vp[512 * i:512 * i + 512, :].rearrange("(p j) f -> p (j f)", j=4))
             vraws[i] = t
 
-        k_load(0)
-        k_load(1)
+        def w_load():
+            for ih in range(2):
+                t = kraw_pool.tile([P, 4096], BF16, name="wraw", tag="kraw")
+                nc.gpsimd.dma_start(out=t[:].rearrange("p (i k) -> p i k", i=4), in_=w_view[:, 4 * ih:4 * ih + 4, :])
+                wraws.append(t)
 
-        qt_ps = psum.tile([P, 512], F32, name="qt_ps", tag="pa")
-        for h in range(H):
-            nc.tensor.transpose(qt_ps[:, 128 * h:128 * h + 128], q_sb[:].bitcast(F32)[:, 128 * h:128 * h + 128], ident_f[:])
-        qT = const.tile([P, 1024], BF16, name="qT")
-        nc.vector.tensor_copy(
-            out=qT[:].rearrange("p (e n) -> p e n", e=2),
-            in_=qt_ps[:].bitcast(BF16).rearrange("p (n e) -> p e n", e=2),
-        )
+        q_sb = s_pool.tile([P, 1024], BF16, name="q_sb", tag="s", align_bytes=64)
+        nc.sync.dma_start(out=q_sb[:], in_=qp)
+        for c in range(KB):
+            k_load(c)
+        nc.scalar.dma_start(out=b_raw[:], in_=out_proj_b.rearrange("(p i) -> p i", i=8))
 
         def k_transpose(c):
             kt = kt_pool.tile([P, 4096], BF16, name="kt", tag="kt")
             kw = kraws[c][:].bitcast(F32)
             for h in range(H):
-                kt_ps = psum.tile([P, 512], F32, name="kt_ps", tag="pa")
+                kt_ps = bank_a([P, 512], F32, "kt_ps") if h < 3 else bank_w([P, 512], F32, "kt_ps")
                 for j in range(4):
                     nc.tensor.transpose(kt_ps[:, 128 * j:128 * j + 128], kw[:, 512 * j + 128 * h:512 * j + 128 * h + 128], ident_f[:])
                 nc.scalar.copy(out=kt[:].bitcast(F32)[:, 512 * h:512 * h + 512], in_=kt_ps[:])
             kts[c] = kt
 
-        def k_scores(c):
-            kv = kts[c][:].rearrange("p (n e) -> p n e", e=2)
+        qT = const.tile([P, 1024], BF16, name="qT")
+
+        def q_prep():
+            qt_ps = psum.tile([P, 512], F32, name="qt_ps", tag="pb")
             for h in range(H):
+                nc.tensor.transpose(qt_ps[:, 128 * h:128 * h + 128], q_sb[:].bitcast(F32)[:, 128 * h:128 * h + 128], ident_f[:])
+            nc.vector.tensor_copy(
+                out=qT[:].rearrange("p (e n) -> p e n", e=2),
+                in_=qt_ps[:].bitcast(BF16).rearrange("p (n e) -> p e n", e=2),
+            )
+            nc.vector.tensor_copy(out=b32[:], in_=b_raw[:])
+
+        def k_scores(c, heads):
+            kv = kts[c][:].rearrange("p (n e) -> p n e", e=2)
+            for h in heads:
                 if c % 2 == 0:
                     s_tiles[(h, c // 2)] = s_pool.tile([P, 1024], F32, name="s_t", tag="s", align_bytes=64)
                 s_ps = psum.tile([P, 512], F32, name="s_ps", tag="pb")
@@ -128,147 +150,196 @@ def tile_pma_pb_t_kernel(tc, qp, kp, vp, out_proj_w, out_proj_b, out):
                     accum_out=mx[:, NCH * h + c:NCH * h + c + 1],
                 )
 
-        def v_prep(i, engines):
-            vc = vc_pool.tile([P, 1024], U32, name="vc", tag="vc", align_bytes=64)
-            vs = vc_pool.tile([P, 1024], U8, name="vs", tag="vs", align_bytes=64)
-            groups = []
-            for u in range(2):
-                g = vgrp_pool.tile([P, 2048], BF16, name="vgrp", tag="vgrp", align_bytes=64)
-                dst = g[:].rearrange("p (c i t) -> p c t i", i=4, t=4)
-                src = vraws[i][:].rearrange("p (t f) -> p t f", t=4)[:, :, 512 * u:512 * u + 512].rearrange(
-                    "p t (c i) -> p c t i", i=4
-                )
-                copy_on(nc, engines[u], dst, src)
-                groups.append(g)
-            for u in range(2):
-                nc.vector.quantize_mx(
-                    out=vc[:, 512 * u:512 * u + 512].bitcast(FP8X4),
-                    scales=vs[:, 512 * u:512 * u + 512],
-                    in_=groups[u][:],
-                )
-            vcs[i] = vc
-            vss[i] = vs
+        state = {"next": 0}
+        pending = []
 
+        def flush_loads():
+            while pending:
+                v_load(pending.pop(0))
+
+        def group(hv, engines):
+            g = vgrp_pool.tile([P, 2048], BF16, name="grp", tag="vgrp", align_bytes=64)
+            grps[hv] = g
+            i, u = hv // 2, hv % 2
+            n = len(engines)
+            w = 512 // n
+            for k in range(n):
+                dst = g[:, 4 * w * k:4 * w * (k + 1)].rearrange("p (c i t) -> p c t i", i=4, t=4)
+                f0 = 512 * u + w * k
+                src = vraws[i][:].rearrange("p (t f) -> p t f", t=4)[:, :, f0:f0 + w].rearrange("p t (c i) -> p c t i", i=4)
+                copy_on(nc, engines[k], dst, src)
+            if u == 1 and i + 2 < NCH:
+                pending.append(i + 2)
+
+        def quant(key, u, g):
+            if u == 0:
+                vcs[key] = vc_pool.tile([P, 1024], U32, name="vc", tag="vc", align_bytes=64)
+                vss[key] = vc_pool.tile([P, 1024], U8, name="vs", tag="vs", align_bytes=64)
+            nc.vector.quantize_mx(
+                out=vcs[key][:, 512 * u:512 * u + 512].bitcast(FP8X4),
+                scales=vss[key][:, 512 * u:512 * u + 512],
+                in_=g[:],
+            )
+
+        def step(engines):
+            k = state["next"]
+            if 1 <= k <= 32:
+                quant((k - 1) // 2, (k - 1) % 2, grps[k - 1])
+            if k < 32:
+                group(k, engines)
+            state["next"] = k + 1
+
+        q_prep()
         k_transpose(0)
         for c in range(NCH):
-            if c + 2 < NCH:
-                k_load(c + 2)
-            if c % 2 == 0:
-                v_load(c // 2)
+            if c < 2:
+                v_load(c)
+            if c + KB < NCH:
+                k_load(c + KB)
+            flush_loads()
+            k_scores(c, (0, 1))
             if c + 1 < NCH:
                 k_transpose(c + 1)
-            k_scores(c)
-            if c % 2 == 1:
-                v_prep(c // 2, ("s", "v"))
-
-        v_load(8)
-        v_load(9)
-        wraws = []
-        w_view = out_proj_w.rearrange("(p i) k -> p i k", i=8)
-        for ih in range(2):
-            t = kraw_pool.tile([P, 4096], BF16, name="wraw", tag="kraw")
-            nc.sync.dma_start(out=t[:].rearrange("p (i k) -> p i k", i=4), in_=w_view[:, 4 * ih:4 * ih + 4, :])
-            wraws.append(t)
+            k_scores(c, (2, 3))
+            if V_LAG <= c < NCH - 1:
+                step(("s", "v"))
 
         nc.vector.tensor_reduce(
             out=negm[:], in_=mx[:].rearrange("p (h c) -> p h c", h=H), axis=AX.X, op=ALU.max, negate=True
         )
+        step(("s",))
+        e_sbs = {}
+        ecs = {}
+        ess = {}
+        egrps = {}
+        et_pss = {}
+        wt_pss = {}
+
+        def e_exp(cc, h):
+            if h == 0:
+                e_sbs[cc] = kt_pool.tile([P, 4096], BF16, name="e_sb", tag="kt")
+            nc.scalar.activation(
+                out=e_sbs[cc][:, 1024 * h:1024 * h + 1024],
+                in_=s_tiles[(h, cc)][:],
+                func=ACT.Exp,
+                bias=negm[:, h:h + 1],
+                scale=1.0,
+                accum_out=rs[:, 8 * h + cc:8 * h + cc + 1],
+            )
+
+        def e_transpose(c, hp):
+            cc, half = c // 2, c % 2
+            et_ps = bank_a([P, 1024], BF16, "et_ps")
+            et_pss[(c, hp)] = et_ps
+            for hh in range(2):
+                h = 2 * hp + hh
+                for t in range(4):
+                    col = 1024 * h + 512 * half + 128 * t
+                    nc.tensor.transpose(
+                        et_ps[:, 512 * hh + 128 * t:512 * hh + 128 * t + 128], e_sbs[cc][:, col:col + 128], ident_b[:]
+                    )
+
+        def e_evac(c, hp, eng):
+            cc, half = c // 2, c % 2
+            if hp == 0:
+                if half == 0:
+                    ecs[cc] = s_pool.tile([P, 1024], U32, name="ec2", tag="s", align_bytes=64)
+                    ess[cc] = s_pool.tile([P, 1024], U8, name="es2", tag="s", align_bytes=64)
+                egrps[c] = s_pool.tile([P, 2048], BF16, name="egrp", tag="s", align_bytes=64)
+            copy_on(
+                nc,
+                eng,
+                egrps[c][:, 1024 * hp:1024 * hp + 1024].rearrange("p (h s t) -> p h s t", h=2, t=4),
+                et_pss[(c, hp)][:].rearrange("p (h t s) -> p h s t", h=2, t=4),
+            )
+
+        def e_quant(c):
+            cc, half = c // 2, c % 2
+            nc.vector.quantize_mx(
+                out=ecs[cc][:, 512 * half:512 * half + 512].bitcast(FP8X4),
+                scales=ess[cc][:, 512 * half:512 * half + 512],
+                in_=egrps[c][:],
+            )
 
         o_ps = []
-        for h in range(H):
-            o_ps.append(psum.tile([P, 512], F32, name="o_ps", tag="pb"))
 
-        wcs = []
-        wss = []
-
-        def w_prep(g):
-            wc = vc_pool.tile([P, 1024], U32, name="wc", tag="vc", align_bytes=64)
-            ws = vc_pool.tile([P, 1024], U8, name="ws", tag="vs", align_bytes=64)
-            for ih in range(2):
-                ww = wraws[ih][:].bitcast(F32)
-                wg = vgrp_pool.tile([P, 2048], BF16, name="wgrp", tag="vgrp", align_bytes=64)
-                for ip in range(2):
-                    wt_ps = psum.tile([P, 512], F32, name="wt_ps", tag="pa")
-                    for i2 in range(2):
-                        il = 2 * ip + i2
-                        for u in range(2):
-                            col = 512 * il + 256 * g + 128 * u
-                            nc.tensor.transpose(
-                                wt_ps[:, 256 * i2 + 128 * u:256 * i2 + 128 * u + 128], ww[:, col:col + 128], ident_f[:]
-                            )
-                    copy_on(
-                        nc,
-                        "s" if ip == 0 else "v",
-                        wg[:].bitcast(F32)[:, 512 * ip:512 * ip + 512].rearrange("q (i p u) -> q i p u", i=2, u=2),
-                        wt_ps[:].rearrange("q (i u p) -> q i p u", i=2, u=2),
-                    )
-                nc.vector.quantize_mx(
-                    out=wc[:, 512 * ih:512 * ih + 512].bitcast(FP8X4),
-                    scales=ws[:, 512 * ih:512 * ih + 512],
-                    in_=wg[:],
-                )
-            wcs.append(wc)
-            wss.append(ws)
-
-        for cc in range(8):
-            e_sb = kt_pool.tile([P, 4096], BF16, name="e_sb", tag="kt")
-            for h in range(H):
-                nc.scalar.activation(
-                    out=e_sb[:, 1024 * h:1024 * h + 1024],
-                    in_=s_tiles[(h, cc)][:],
-                    func=ACT.Exp,
-                    bias=negm[:, h:h + 1],
-                    scale=1.0,
-                    accum_out=rs[:, 8 * h + cc:8 * h + cc + 1],
-                )
-            ec2 = s_pool.tile([P, 1024], U32, name="ec2", tag="s", align_bytes=64)
-            es2 = s_pool.tile([P, 1024], U8, name="es2", tag="s", align_bytes=64)
-            for half in range(2):
-                c = 2 * cc + half
-                egrp = s_pool.tile([P, 2048], BF16, name="egrp", tag="s", align_bytes=64)
-                for hp in range(2):
-                    et_ps = psum.tile([P, 1024], BF16, name="et_ps", tag="pa")
-                    for hh in range(2):
-                        h = 2 * hp + hh
-                        for t in range(4):
-                            col = 1024 * h + 512 * half + 128 * t
-                            nc.tensor.transpose(
-                                et_ps[:, 512 * hh + 128 * t:512 * hh + 128 * t + 128], e_sb[:, col:col + 128], ident_b[:]
-                            )
-                    copy_on(
-                        nc,
-                        "s" if hp == 0 else "v",
-                        egrp[:, 1024 * hp:1024 * hp + 1024].rearrange("p (h s t) -> p h s t", h=2, t=4),
-                        et_ps[:].rearrange("p (h t s) -> p h s t", h=2, t=4),
-                    )
-                nc.vector.quantize_mx(
-                    out=ec2[:, 512 * half:512 * half + 512].bitcast(FP8X4),
-                    scales=es2[:, 512 * half:512 * half + 512],
-                    in_=egrp[:],
-                )
+        def pv(c):
+            cc, half = c // 2, c % 2
+            if c == 0:
                 for h in range(H):
-                    ecol = 512 * half + 128 * h
-                    nc.tensor.matmul_mx(
-                        out=o_ps[h][:, 0:256],
-                        lhsT=ec2[:, ecol:ecol + 128].bitcast(FP8X4),
-                        lhsT_scale=es2[:, ecol:ecol + 128],
-                        rhs=vcs[c][:, 256 * h:256 * h + 256].bitcast(FP8X4),
-                        rhs_scale=vss[c][:, 256 * h:256 * h + 256],
-                        start=(c == 0),
-                        stop=(c == NCH - 1),
-                    )
-                if half == 0:
-                    v_prep(8 + cc, ("v", "v"))
-                    if 8 + cc + 2 < NCH:
-                        v_load(8 + cc + 2)
-            if cc == 5:
-                w_prep(0)
-            if cc == 6:
-                w_prep(1)
+                    o_ps.append(psum.tile([P, 512], F32, name="o_ps", tag="pb"))
+            for h in range(H):
+                ecol = 512 * half + 128 * h
+                nc.tensor.matmul_mx(
+                    out=o_ps[h][:, 0:256],
+                    lhsT=ecs[cc][:, ecol:ecol + 128].bitcast(FP8X4),
+                    lhsT_scale=ess[cc][:, ecol:ecol + 128],
+                    rhs=vcs[c][:, 256 * h:256 * h + 256].bitcast(FP8X4),
+                    rhs_scale=vss[c][:, 256 * h:256 * h + 256],
+                    start=(c == 0),
+                    stop=(c == NCH - 1),
+                )
 
-        nc.vector.tensor_reduce(out=rsum[:], in_=rs[:].rearrange("p (h c) -> p h c", h=H), axis=AX.X, op=ALU.add)
-        nc.vector.reciprocal(out=rinv[:], in_=rsum[:])
-        o_sb = const.tile([P, 1024], BF16, name="o_sb")
+        def w_transpose(wb):
+            gg, ih, ip = wb // 4, (wb // 2) % 2, wb % 2
+            ww = wraws[ih][:].bitcast(F32)
+            wt_ps = bank_w([P, 512], F32, "wt_ps")
+            wt_pss[wb] = wt_ps
+            for i2 in range(2):
+                il = 2 * ip + i2
+                for u in range(2):
+                    col = 512 * il + 256 * gg + 128 * u
+                    nc.tensor.transpose(wt_ps[:, 256 * i2 + 128 * u:256 * i2 + 128 * u + 128], ww[:, col:col + 128], ident_f[:])
+
+        def w_evac(wb):
+            gg, ih, ip = wb // 4, (wb // 2) % 2, wb % 2
+            if ip == 0:
+                grps[("w", gg, ih)] = s_pool.tile([P, 2048], BF16, name="wgrp", tag="s", align_bytes=64)
+            copy_on(
+                nc,
+                "s" if ip == 0 else "v",
+                grps[("w", gg, ih)][:].bitcast(F32)[:, 512 * ip:512 * ip + 512].rearrange("q (i p u) -> q i p u", i=2, u=2),
+                wt_pss[wb][:].rearrange("q (i u p) -> q i p u", i=2, u=2),
+            )
+
+        for h in range(H):
+            e_exp(0, h)
+        w_load()
+        for k in range(FILL_STEPS):
+            flush_loads()
+            step(("v",))
+        e_transpose(0, 0)
+        e_transpose(0, 1)
+        for c in range(NCH):
+            cc = c // 2
+            flush_loads()
+            if cc + 1 < 8:
+                e_exp(cc + 1, 2 * (c % 2))
+                e_exp(cc + 1, 2 * (c % 2) + 1)
+            if c + 1 < NCH:
+                e_transpose(c + 1, 0)
+            e_evac(c, 0, "v" if c < 14 else "s")
+            if c + 1 < NCH:
+                e_transpose(c + 1, 1)
+            e_evac(c, 1, "s")
+            wb = c - W_FIRST
+            if 1 <= wb <= 8:
+                w_evac(wb - 1)
+            if 0 <= wb <= 7:
+                w_transpose(wb)
+            step(("v",))
+            if c in DOUBLE:
+                step(("v",))
+            if c == 14:
+                nc.vector.tensor_reduce(out=rsum[:], in_=rs[:].rearrange("p (h c) -> p h c", h=H), axis=AX.X, op=ALU.add)
+                nc.vector.reciprocal(out=rinv[:], in_=rsum[:])
+            if 3 <= wb <= 9 and wb % 2 == 1:
+                gg, ih = (wb - 3) // 4, ((wb - 3) // 2) % 2
+                quant("w%d" % gg, ih, grps[("w", gg, ih)])
+            e_quant(c)
+            pv(c)
+
+        o_sb = s_pool.tile([P, 1024], BF16, name="o_sb", tag="s", align_bytes=64)
         for h in range(H):
             dst = o_sb[:, 256 * h:256 * h + 256].rearrange("s (e p) -> s e p", e=2)
             src = o_ps[h][:, 0:256].rearrange("s (p e) -> s e p", e=2)
@@ -276,10 +347,10 @@ def tile_pma_pb_t_kernel(tc, qp, kp, vp, out_proj_w, out_proj_b, out):
                 nc.vector.tensor_scalar(out=dst, in0=src, scalar1=rinv[:, h:h + 1], scalar2=None, op0=ALU.mult)
             else:
                 nc.scalar.activation(out=dst, in_=src, func=ACT.Copy, scale=rinv[:, h:h + 1])
-        ot_ps = psum.tile([P, 1024], BF16, name="ot_ps", tag="pa")
+        ot_ps = bank_a([P, 1024], BF16, "ot_ps")
         for b8 in range(8):
             nc.tensor.transpose(ot_ps[:, 128 * b8:128 * b8 + 128], o_sb[:, 128 * b8:128 * b8 + 128], ident_b[:])
-        ogrp = const.tile([P, 1024], BF16, name="ogrp", align_bytes=64)
+        ogrp = s_pool.tile([P, 1024], BF16, name="ogrp", tag="s", align_bytes=64)
         for g in range(2):
             copy_on(
                 nc,
@@ -287,18 +358,18 @@ def tile_pma_pb_t_kernel(tc, qp, kp, vp, out_proj_w, out_proj_b, out):
                 ogrp[:, 512 * g:512 * g + 512].rearrange("p (s t) -> p s t", t=4),
                 ot_ps[:, 512 * g:512 * g + 512].rearrange("p (t s) -> p s t", t=4),
             )
-        oc = const.tile([P, 256], U32, name="oc", align_bytes=64)
-        osc = const.tile([P, 256], U8, name="osc", align_bytes=64)
+        oc = s_pool.tile([P, 256], U32, name="oc", tag="s", align_bytes=64)
+        osc = s_pool.tile([P, 256], U8, name="osc", tag="s", align_bytes=64)
         nc.vector.quantize_mx(out=oc[:].bitcast(FP8X4), scales=osc[:], in_=ogrp[:])
         for b in range(2):
-            y_ps = psum.tile([P, 512], F32, name="y_ps", tag="pa")
+            y_ps = bank_a([P, 512], F32, "y_ps")
             for i4 in range(4):
                 i = 4 * b + i4
                 for g in range(2):
                     nc.tensor.matmul_mx(
                         out=y_ps[:, 128 * i4:128 * i4 + 128],
-                        lhsT=wcs[g][:, 128 * i:128 * i + 128].bitcast(FP8X4),
-                        lhsT_scale=wss[g][:, 128 * i:128 * i + 128],
+                        lhsT=vcs["w%d" % g][:, 128 * i:128 * i + 128].bitcast(FP8X4),
+                        lhsT_scale=vss["w%d" % g][:, 128 * i:128 * i + 128],
                         rhs=oc[:, 128 * g:128 * g + 128].bitcast(FP8X4),
                         rhs_scale=osc[:, 128 * g:128 * g + 128],
                         start=(g == 0),

@@ -15,11 +15,11 @@ AX = mybir.AxisListType
 P = 128
 H = 4
 NCH = 16
-NV = 8
+NV = 5
 KB = 3
-V_LAG = 1
-FILL_STEPS = 1
-DOUBLE = (1, 2)
+VB = 3
+EV_V = (7, 14, 15)
+FILL_STEPS = 4
 W_FIRST = 3
 
 FLOPS = 2 * 128 * 8192 * 1024 * 2 + 2 * 128 * 1024 * 1024
@@ -40,9 +40,9 @@ def tile_pma_pb_t_kernel(tc, qp, kp, vp, out_proj_w, out_proj_b, out):
         const = ctx.enter_context(tc.tile_pool(name="const", bufs=1))
         s_pool = ctx.enter_context(tc.tile_pool(name="s_pool", bufs=32))
         kraw_pool = ctx.enter_context(tc.tile_pool(name="kraw_pool", bufs=KB))
-        vraw_pool = ctx.enter_context(tc.tile_pool(name="vraw_pool", bufs=2))
+        vraw_pool = ctx.enter_context(tc.tile_pool(name="vraw_pool", bufs=VB))
         kt_pool = ctx.enter_context(tc.tile_pool(name="kt_pool", bufs=2))
-        vgrp_pool = ctx.enter_context(tc.tile_pool(name="vgrp_pool", bufs=2))
+        vgrp_pool = ctx.enter_context(tc.tile_pool(name="vgrp_pool", bufs=3))
         vc_pool = ctx.enter_context(tc.tile_pool(name="vc_pool", bufs=NV))
         psum = ctx.enter_context(tc.psum_pool(name="psum", bufs=4))
         ctx.enter_context(tc.manual_schedule())
@@ -89,13 +89,13 @@ def tile_pma_pb_t_kernel(tc, qp, kp, vp, out_proj_w, out_proj_b, out):
 
         def v_load(i):
             t = vraw_pool.tile([P, 4096], BF16, name="vraw", tag="vraw")
-            (nc.sync if i < 2 else nc.gpsimd).dma_start(out=t[:], in_=vp[512 * i:512 * i + 512, :].rearrange("(p j) f -> p (j f)", j=4))
+            nc.sync.dma_start(out=t[:], in_=vp[512 * i:512 * i + 512, :].rearrange("(p j) f -> p (j f)", j=4))
             vraws[i] = t
 
         def w_load():
             for ih in range(2):
                 t = kraw_pool.tile([P, 4096], BF16, name="wraw", tag="kraw")
-                nc.gpsimd.dma_start(out=t[:].rearrange("p (i k) -> p i k", i=4), in_=w_view[:, 4 * ih:4 * ih + 4, :])
+                nc.sync.dma_start(out=t[:].rearrange("p (i k) -> p i k", i=4), in_=w_view[:, 4 * ih:4 * ih + 4, :])
                 wraws.append(t)
 
         q_sb = s_pool.tile([P, 1024], BF16, name="q_sb", tag="s", align_bytes=64)
@@ -126,12 +126,18 @@ def tile_pma_pb_t_kernel(tc, qp, kp, vp, out_proj_w, out_proj_b, out):
             )
             nc.vector.tensor_copy(out=b32[:], in_=b_raw[:])
 
-        def k_scores(c, heads):
+        def round1(c):
             kv = kts[c][:].rearrange("p (n e) -> p n e", e=2)
-            for h in heads:
+            more = c + 1 < NCH
+            if more:
+                kts[c + 1] = kt_pool.tile([P, 4096], BF16, name="kt", tag="kt")
+                kw = kraws[c + 1][:].bitcast(F32)
+            for h in range(H):
                 if c % 2 == 0:
                     s_tiles[(h, c // 2)] = s_pool.tile([P, 1024], F32, name="s_t", tag="s", align_bytes=64)
                 s_ps = psum.tile([P, 512], F32, name="s_ps", tag="pb")
+                if more:
+                    kt_ps = bank_a([P, 512], F32, "kt_ps") if h < 3 else bank_w([P, 512], F32, "kt_ps")
                 for e in range(2):
                     nc.tensor.matmul(
                         out=s_ps[:],
@@ -140,6 +146,13 @@ def tile_pma_pb_t_kernel(tc, qp, kp, vp, out_proj_w, out_proj_b, out):
                         start=(e == 0),
                         stop=(e == 1),
                     )
+                    if more:
+                        for j in (2 * e, 2 * e + 1):
+                            nc.tensor.transpose(
+                                kt_ps[:, 128 * j:128 * j + 128], kw[:, 512 * j + 128 * h:512 * j + 128 * h + 128], ident_f[:]
+                            )
+                if more:
+                    nc.scalar.copy(out=kts[c + 1][:].bitcast(F32)[:, 512 * h:512 * h + 512], in_=kt_ps[:])
                 nc.vector.tensor_scalar(
                     out=s_tiles[(h, c // 2)][:, 512 * (c % 2):512 * (c % 2) + 512],
                     in0=s_ps[:],
@@ -168,8 +181,8 @@ def tile_pma_pb_t_kernel(tc, qp, kp, vp, out_proj_w, out_proj_b, out):
                 f0 = 512 * u + w * k
                 src = vraws[i][:].rearrange("p (t f) -> p t f", t=4)[:, :, f0:f0 + w].rearrange("p t (c i) -> p c t i", i=4)
                 copy_on(nc, engines[k], dst, src)
-            if u == 1 and i + 2 < NCH:
-                pending.append(i + 2)
+            if u == 1 and i + VB < NCH:
+                pending.append(i + VB)
 
         def quant(key, u, g):
             if u == 0:
@@ -192,22 +205,15 @@ def tile_pma_pb_t_kernel(tc, qp, kp, vp, out_proj_w, out_proj_b, out):
         q_prep()
         k_transpose(0)
         for c in range(NCH):
-            if c < 2:
-                v_load(c)
             if c + KB < NCH:
                 k_load(c + KB)
-            flush_loads()
-            k_scores(c, (0, 1))
-            if c + 1 < NCH:
-                k_transpose(c + 1)
-            k_scores(c, (2, 3))
-            if V_LAG <= c < NCH - 1:
-                step(("s", "v"))
+            elif c + KB < NCH + VB:
+                v_load(c + KB - NCH)
+            round1(c)
 
         nc.vector.tensor_reduce(
             out=negm[:], in_=mx[:].rearrange("p (h c) -> p h c", h=H), axis=AX.X, op=ALU.max, negate=True
         )
-        step(("s",))
         e_sbs = {}
         ecs = {}
         ess = {}
@@ -318,18 +324,18 @@ def tile_pma_pb_t_kernel(tc, qp, kp, vp, out_proj_w, out_proj_b, out):
                 e_exp(cc + 1, 2 * (c % 2) + 1)
             if c + 1 < NCH:
                 e_transpose(c + 1, 0)
-            e_evac(c, 0, "v" if c < 14 else "s")
+            e_evac(c, 0, "s")
             if c + 1 < NCH:
                 e_transpose(c + 1, 1)
-            e_evac(c, 1, "s")
+            e_evac(c, 1, "v" if c in EV_V else "s")
             wb = c - W_FIRST
             if 1 <= wb <= 8:
                 w_evac(wb - 1)
             if 0 <= wb <= 7:
                 w_transpose(wb)
             step(("v",))
-            if c in DOUBLE:
-                step(("v",))
+            flush_loads()
+            step(("v",))
             if c == 14:
                 nc.vector.tensor_reduce(out=rsum[:], in_=rs[:].rearrange("p (h c) -> p h c", h=H), axis=AX.X, op=ALU.add)
                 nc.vector.reciprocal(out=rinv[:], in_=rsum[:])

@@ -45,7 +45,6 @@ def tile_pma_pb_t_kernel(tc, qp, kp, vp, out_proj_w, out_proj_b, out):
         vgrp_pool = ctx.enter_context(tc.tile_pool(name="vgrp_pool", bufs=3))
         vc_pool = ctx.enter_context(tc.tile_pool(name="vc_pool", bufs=NV))
         psum = ctx.enter_context(tc.psum_pool(name="psum", bufs=4))
-        ctx.enter_context(tc.manual_schedule())
 
         def bank_a(shape, dtype, name):
             return psum.tile(shape, dtype, name=name, tag="pa", bufs=3)

@@ -19,7 +19,7 @@ NV = 5
 KB = 3
 VB = 3
 EV_V = (7, 14, 15)
-FILL_STEPS = 4
+FILL_STEPS = 2
 W_FIRST = 3
 
 FLOPS = 2 * 128 * 8192 * 1024 * 2 + 2 * 128 * 1024 * 1024
@@ -42,9 +42,10 @@ def tile_pma_pb_t_kernel(tc, qp, kp, vp, out_proj_w, out_proj_b, out):
         kraw_pool = ctx.enter_context(tc.tile_pool(name="kraw_pool", bufs=KB))
         vraw_pool = ctx.enter_context(tc.tile_pool(name="vraw_pool", bufs=VB))
         kt_pool = ctx.enter_context(tc.tile_pool(name="kt_pool", bufs=2))
-        vgrp_pool = ctx.enter_context(tc.tile_pool(name="vgrp_pool", bufs=3))
+        vgrp_pool = ctx.enter_context(tc.tile_pool(name="vgrp_pool", bufs=2))
         vc_pool = ctx.enter_context(tc.tile_pool(name="vc_pool", bufs=NV))
         psum = ctx.enter_context(tc.psum_pool(name="psum", bufs=4))
+        ctx.enter_context(tc.manual_schedule())
 
         def bank_a(shape, dtype, name):
             return psum.tile(shape, dtype, name=name, tag="pa", bufs=3)
@@ -169,19 +170,20 @@ def tile_pma_pb_t_kernel(tc, qp, kp, vp, out_proj_w, out_proj_b, out):
             while pending:
                 v_load(pending.pop(0))
 
-        def group(hv, engines):
-            g = vgrp_pool.tile([P, 2048], BF16, name="grp", tag="vgrp", align_bytes=64)
-            grps[hv] = g
-            i, u = hv // 2, hv % 2
-            n = len(engines)
-            w = 512 // n
-            for k in range(n):
-                dst = g[:, 4 * w * k:4 * w * (k + 1)].rearrange("p (c i t) -> p c t i", i=4, t=4)
-                f0 = 512 * u + w * k
-                src = vraws[i][:].rearrange("p (t f) -> p t f", t=4)[:, :, f0:f0 + w].rearrange("p t (c i) -> p c t i", i=4)
-                copy_on(nc, engines[k], dst, src)
-            if u == 1 and i + VB < NCH:
+        def group(i):
+            g = vgrp_pool.tile([P, 4096], BF16, name="grp", tag="vgrp", align_bytes=64)
+            grps[i] = g
+            nc.vector.tensor_copy(
+                out=g[:].rearrange("p (c i t) -> p c t i", i=4, t=4),
+                in_=vraws[i][:].rearrange("p (t c i) -> p c t i", t=4, i=4),
+            )
+            if i + VB < NCH:
                 pending.append(i + VB)
+
+        def v_quant(i):
+            vcs[i] = vc_pool.tile([P, 1024], U32, name="vc", tag="vc", align_bytes=64)
+            vss[i] = vc_pool.tile([P, 1024], U8, name="vs", tag="vs", align_bytes=64)
+            nc.vector.quantize_mx(out=vcs[i][:].bitcast(FP8X4), scales=vss[i][:], in_=grps[i][:])
 
         def quant(key, u, g):
             if u == 0:
@@ -193,12 +195,12 @@ def tile_pma_pb_t_kernel(tc, qp, kp, vp, out_proj_w, out_proj_b, out):
                 in_=g[:],
             )
 
-        def step(engines):
+        def step():
             k = state["next"]
-            if 1 <= k <= 32:
-                quant((k - 1) // 2, (k - 1) % 2, grps[k - 1])
-            if k < 32:
-                group(k, engines)
+            if 1 <= k <= NCH:
+                v_quant(k - 1)
+            if k < NCH:
+                group(k)
             state["next"] = k + 1
 
         q_prep()
@@ -312,7 +314,7 @@ def tile_pma_pb_t_kernel(tc, qp, kp, vp, out_proj_w, out_proj_b, out):
         w_load()
         for k in range(FILL_STEPS):
             flush_loads()
-            step(("v",))
+            step()
         e_transpose(0, 0)
         e_transpose(0, 1)
         for c in range(NCH):
@@ -332,9 +334,7 @@ def tile_pma_pb_t_kernel(tc, qp, kp, vp, out_proj_w, out_proj_b, out):
                 w_evac(wb - 1)
             if 0 <= wb <= 7:
                 w_transpose(wb)
-            step(("v",))
-            flush_loads()
-            step(("v",))
+            step()
             if c == 14:
                 nc.vector.tensor_reduce(out=rsum[:], in_=rs[:].rearrange("p (h c) -> p h c", h=H), axis=AX.X, op=ALU.add)
                 nc.vector.reciprocal(out=rinv[:], in_=rsum[:])

from contextlib import ExitStack

import concourse.mybir as mybir
from concourse.masks import make_identity

F32 = mybir.dt.float32
BF16 = mybir.dt.bfloat16
U8 = mybir.dt.uint8
U32 = mybir.dt.uint32
FP8X4 = mybir.dt.float8_e4m3fn_x4
ALU = mybir.AluOpType
ACT = mybir.ActivationFunctionType
AX = mybir.AxisListType

P = 128
H = 4
NCH = 16
NV = 5
KB = 3
VB = 3
EV_V = (7, 14, 15)
FILL_STEPS = 2
W_FIRST = 3

FLOPS = 2 * 128 * 8192 * 1024 * 2 + 2 * 128 * 1024 * 1024


def copy_on(nc, eng, out, in_):
    if eng == "v":
        nc.vector.tensor_copy(out=out, in_=in_)
    elif eng == "s":
        nc.scalar.copy(out=out, in_=in_)
    else:
        nc.gpsimd.tensor_scalar(out=out, in0=in_, scalar1=1.0, scalar2=0.0, op0=ALU.mult, op1=ALU.add)


def tile_pma_pb_t_kernel(tc, qp, kp, vp, out_proj_w, out_proj_b, out):
    nc = tc.nc
    with ExitStack() as ctx:
        const = ctx.enter_context(tc.tile_pool(name="const", bufs=1))
        s_pool = ctx.enter_context(tc.tile_pool(name="s_pool", bufs=32))
        kraw_pool = ctx.enter_context(tc.tile_pool(name="kraw_pool", bufs=KB))
        vraw_pool = ctx.enter_context(tc.tile_pool(name="vraw_pool", bufs=VB))
        kt_pool = ctx.enter_context(tc.tile_pool(name="kt_pool", bufs=2))
        vgrp_pool = ctx.enter_context(tc.tile_pool(name="vgrp_pool", bufs=2))
        vc_pool = ctx.enter_context(tc.tile_pool(name="vc_pool", bufs=NV))
        psum = ctx.enter_context(tc.psum_pool(name="psum", bufs=4))
        ctx.enter_context(tc.manual_schedule())

        def bank_a(shape, dtype, name):
            return psum.tile(shape, dtype, name=name, tag="pa", bufs=3)

        def bank_w(shape, dtype, name):
            return psum.tile(shape, dtype, name=name, tag="pw", bufs=1)

        ident_f = const.tile([P, P], F32, name="ident_f")
        make_identity(nc, ident_f[:])
        ident_b = const.tile([P, P], BF16, name="ident_b")
        make_identity(nc, ident_b[:])
        warm = const.tile([P, 1], F32, name="warm")
        nc.vector.memset(warm[:], 0.0)
        warm2 = const.tile([P, 1], F32, name="warm2")
        nc.scalar.activation(out=warm2[:], in_=warm[:], func=ACT.Exp)

        mx = const.tile([P, H * NCH], F32, name="mx")
        negm = const.tile([P, H], F32, name="negm")
        rs = const.tile([P, H * 8], F32, name="rs")
        rsum = const.tile([P, H], F32, name="rsum")
        rinv = const.tile([P, H], F32, name="rinv")
        b_raw = const.tile([P, 8], BF16, name="b_raw")
        b32 = const.tile([P, 8], F32, name="b32")
        ysum = const.tile([P, 8], F32, name="ysum")
        res = const.tile([P, 8], F32, name="res")

        kraws = {}
        vraws = {}
        kts = {}
        vcs = {}
        vss = {}
        grps = {}
        s_tiles = {}
        wraws = []
        w_view = out_proj_w.rearrange("(p i) k -> p i k", i=8)

        def k_load(c):
            t = kraw_pool.tile([P, 4096], BF16, name="kraw", tag="kraw")
            nc.sync.dma_start(out=t[:], in_=kp[512 * c:512 * c + 512, :].rearrange("(p j) f -> p (j f)", j=4))
            kraws[c] = t

        def v_load(i):
            t = vraw_pool.tile([P, 4096], BF16, name="vraw", tag="vraw")
            nc.sync.dma_start(out=t[:], in_=vp[512 * i:512 * i + 512, :].rearrange("(p j) f -> p (j f)", j=4))
            vraws[i] = t

        def w_load():
            for ih in range(2):
                t = kraw_pool.tile([P, 4096], BF16, name="wraw", tag="kraw")
                nc.sync.dma_start(out=t[:].rearrange("p (i k) -> p i k", i=4), in_=w_view[:, 4 * ih:4 * ih + 4, :])
                wraws.append(t)

        q_sb = s_pool.tile([P, 1024], BF16, name="q_sb", tag="s", align_bytes=64)
        nc.sync.dma_start(out=q_sb[:], in_=qp)
        for c in range(KB):
            k_load(c)
        nc.scalar.dma_start(out=b_raw[:], in_=out_proj_b.rearrange("(p i) -> p i", i=8))

        def k_transpose(c):
            kt = kt_pool.tile([P, 4096], BF16, name="kt", tag="kt")
            kw = kraws[c][:].bitcast(F32)
            for h in range(H):
                kt_ps = bank_a([P, 512], F32, "kt_ps") if h < 3 else bank_w([P, 512], F32, "kt_ps")
                for j in range(4):
                    nc.tensor.transpose(kt_ps[:, 128 * j:128 * j + 128], kw[:, 512 * j + 128 * h:512 * j + 128 * h + 128], ident_f[:])
                nc.scalar.copy(out=kt[:].bitcast(F32)[:, 512 * h:512 * h + 512], in_=kt_ps[:])
            kts[c] = kt

        qT = const.tile([P, 1024], BF16, name="qT")

        def q_prep():
            qt_ps = psum.tile([P, 512], F32, name="qt_ps", tag="pb")
            for h in range(H):
                nc.tensor.transpose(qt_ps[:, 128 * h:128 * h + 128], q_sb[:].bitcast(F32)[:, 128 * h:128 * h + 128], ident_f[:])
            nc.vector.tensor_copy(
                out=qT[:].rearrange("p (e n) -> p e n", e=2),
                in_=qt_ps[:].bitcast(BF16).rearrange("p (n e) -> p e n", e=2),
            )
            nc.vector.tensor_copy(out=b32[:], in_=b_raw[:])

        def round1(c):
            kv = kts[c][:].rearrange("p (n e) -> p n e", e=2)
            more = c + 1 < NCH
            if more:
                kts[c + 1] = kt_pool.tile([P, 4096], BF16, name="kt", tag="kt")
                kw = kraws[c + 1][:].bitcast(F32)
            for h in range(H):
                if c % 2 == 0:
                    s_tiles[(h, c // 2)] = s_pool.tile([P, 1024], F32, name="s_t", tag="s", align_bytes=64)
                s_ps = psum.tile([P, 512], F32, name="s_ps", tag="pb")
                if more:
                    kt_ps = bank_a([P, 512], F32, "kt_ps") if h < 3 else bank_w([P, 512], F32, "kt_ps")
                for e in range(2):
                    nc.tensor.matmul(
                        out=s_ps[:],
                        lhsT=qT[:, 512 * e + 128 * h:512 * e + 128 * h + 128],
                        rhs=kv[:, 512 * h:512 * h + 512, e],
                        start=(e == 0),
                        stop=(e == 1),
                    )
                    if more:
                        for j in (2 * e, 2 * e + 1):
                            nc.tensor.transpose(
                                kt_ps[:, 128 * j:128 * j + 128], kw[:, 512 * j + 128 * h:512 * j + 128 * h + 128], ident_f[:]
                            )
                if more:
                    nc.scalar.copy(out=kts[c + 1][:].bitcast(F32)[:, 512 * h:512 * h + 512], in_=kt_ps[:])
                nc.vector.tensor_scalar(
                    out=s_tiles[(h, c // 2)][:, 512 * (c % 2):512 * (c % 2) + 512],
                    in0=s_ps[:],
                    scalar1=1.0,
                    scalar2=None,
                    op0=ALU.mult,
                    op1=ALU.max,
                    accum_out=mx[:, NCH * h + c:NCH * h + c + 1],
                )

        state = {"next": 0}
        pending = []

        def flush_loads():
            while pending:
                v_load(pending.pop(0))

        def group(i):
            g = vgrp_pool.tile([P, 4096], BF16, name="grp", tag="vgrp", align_bytes=64)
            grps[i] = g
            nc.vector.tensor_copy(
                out=g[:].rearrange("p (c i t) -> p c t i", i=4, t=4),
                in_=vraws[i][:].rearrange("p (t c i) -> p c t i", t=4, i=4),
            )
            if i + VB < NCH:
                pending.append(i + VB)

        def v_quant(i):
            vcs[i] = vc_pool.tile([P, 1024], U32, name="vc", tag="vc", align_bytes=64)
            vss[i] = vc_pool.tile([P, 1024], U8, name="vs", tag="vs", align_bytes=64)
            nc.vector.quantize_mx(out=vcs[i][:].bitcast(FP8X4), scales=vss[i][:], in_=grps[i][:])

        def quant(key, u, g):
            if u == 0:
                vcs[key] = vc_pool.tile([P, 1024], U32, name="vc", tag="vc", align_bytes=64)
                vss[key] = vc_pool.tile([P, 1024], U8, name="vs", tag="vs", align_bytes=64)
            nc.vector.quantize_mx(
                out=vcs[key][:, 512 * u:512 * u + 512].bitcast(FP8X4),
                scales=vss[key][:, 512 * u:512 * u + 512],
                in_=g[:],
            )

        def step():
            k = state["next"]
            if 1 <= k <= NCH:
                v_quant(k - 1)
            if k < NCH:
                group(k)
            state["next"] = k + 1

        q_prep()
        k_transpose(0)
        for c in range(NCH):
            if c + KB < NCH:
                k_load(c + KB)
            elif c + KB < NCH + VB:
                v_load(c + KB - NCH)
            round1(c)

        nc.vector.tensor_reduce(
            out=negm[:], in_=mx[:].rearrange("p (h c) -> p h c", h=H), axis=AX.X, op=ALU.max, negate=True
        )
        e_sbs = {}
        ecs = {}
        ess = {}
        egrps = {}
        et_pss = {}
        wt_pss = {}

        def e_exp(cc, h):
            if h == 0:
                e_sbs[cc] = kt_pool.tile([P, 4096], BF16, name="e_sb", tag="kt")
            nc.scalar.activation(
                out=e_sbs[cc][:, 1024 * h:1024 * h + 1024],
                in_=s_tiles[(h, cc)][:],
                func=ACT.Exp,
                bias=negm[:, h:h + 1],
                scale=1.0,
                accum_out=rs[:, 8 * h + cc:8 * h + cc + 1],
            )

        def e_transpose(c, hp):
            cc, half = c // 2, c % 2
            et_ps = bank_a([P, 1024], BF16, "et_ps")
            et_pss[(c, hp)] = et_ps
            for hh in range(2):
                h = 2 * hp + hh
                for t in range(4):
                    col = 1024 * h + 512 * half + 128 * t
                    nc.tensor.transpose(
                        et_ps[:, 512 * hh + 128 * t:512 * hh + 128 * t + 128], e_sbs[cc][:, col:col + 128], ident_b[:]
                    )

        def e_evac(c, hp, eng):
            cc, half = c // 2, c % 2
            if hp == 0:
                if half == 0:
                    ecs[cc] = s_pool.tile([P, 1024], U32, name="ec2", tag="s", align_bytes=64)
                    ess[cc] = s_pool.tile([P, 1024], U8, name="es2", tag="s", align_bytes=64)
                egrps[c] = s_pool.tile([P, 2048], BF16, name="egrp", tag="s", align_bytes=64)
            copy_on(
                nc,
                eng,
                egrps[c][:, 1024 * hp:1024 * hp + 1024].rearrange("p (h s t) -> p h s t", h=2, t=4),
                et_pss[(c, hp)][:].rearrange("p (h t s) -> p h s t", h=2, t=4),
            )

        def e_quant(c):
            cc, half = c // 2, c % 2
            nc.vector.quantize_mx(
                out=ecs[cc][:, 512 * half:512 * half + 512].bitcast(FP8X4),
                scales=ess[cc][:, 512 * half:512 * half + 512],
                in_=egrps[c][:],
            )

        o_ps = []

        def pv(c):
            cc, half = c // 2, c % 2
            if c == 0:
                for h in range(H):
                    o_ps.append(psum.tile([P, 512], F32, name="o_ps", tag="pb"))
            for h in range(H):
                ecol = 512 * half + 128 * h
                nc.tensor.matmul_mx(
                    out=o_ps[h][:, 0:256],
                    lhsT=ecs[cc][:, ecol:ecol + 128].bitcast(FP8X4),
                    lhsT_scale=ess[cc][:, ecol:ecol + 128],
                    rhs=vcs[c][:, 256 * h:256 * h + 256].bitcast(FP8X4),
                    rhs_scale=vss[c][:, 256 * h:256 * h + 256],
                    start=(c == 0),
                    stop=(c == NCH - 1),
                )

        def w_transpose(wb):
            gg, ih, ip = wb // 4, (wb // 2) % 2, wb % 2
            ww = wraws[ih][:].bitcast(F32)
            wt_ps = bank_w([P, 512], F32, "wt_ps")
            wt_pss[wb] = wt_ps
            for i2 in range(2):
                il = 2 * ip + i2
                for u in range(2):
                    col = 512 * il + 256 * gg + 128 * u
                    nc.tensor.transpose(wt_ps[:, 256 * i2 + 128 * u:256 * i2 + 128 * u + 128], ww[:, col:col + 128], ident_f[:])

        def w_evac(wb):
            gg, ih, ip = wb // 4, (wb // 2) % 2, wb % 2
            if ip == 0:
                grps[("w", gg, ih)] = s_pool.tile([P, 2048], BF16, name="wgrp", tag="s", align_bytes=64)
            copy_on(
                nc,
                "s" if ip == 0 else "v",
                grps[("w", gg, ih)][:].bitcast(F32)[:, 512 * ip:512 * ip + 512].rearrange("q (i p u) -> q i p u", i=2, u=2),
                wt_pss[wb][:].rearrange("q (i u p) -> q i p u", i=2, u=2),
            )

        for h in range(H):
            e_exp(0, h)
        w_load()
        for k in range(FILL_STEPS):
            flush_loads()
            step()
        e_transpose(0, 0)
        e_transpose(0, 1)
        for c in range(NCH):
            cc = c // 2
            flush_loads()
            if cc + 1 < 8:
                e_exp(cc + 1, 2 * (c % 2))
                e_exp(cc + 1, 2 * (c % 2) + 1)
            if c + 1 < NCH:
                e_transpose(c + 1, 0)
            e_evac(c, 0, "s")
            if c + 1 < NCH:
                e_transpose(c + 1, 1)
            e_evac(c, 1, "v" if c in EV_V else "s")
            wb = c - W_FIRST
            if 1 <= wb <= 8:
                w_evac(wb - 1)
            if 0 <= wb <= 7:
                w_transpose(wb)
            step()
            if c == 14:
                nc.vector.tensor_reduce(out=rsum[:], in_=rs[:].rearrange("p (h c) -> p h c", h=H), axis=AX.X, op=ALU.add)
                nc.vector.reciprocal(out=rinv[:], in_=rsum[:])
            if 3 <= wb <= 9 and wb % 2 == 1:
                gg, ih = (wb - 3) // 4, ((wb - 3) // 2) % 2
                quant("w%d" % gg, ih, grps[("w", gg, ih)])
            e_quant(c)
            pv(c)

        o_sb = s_pool.tile([P, 1024], BF16, name="o_sb", tag="s", align_bytes=64)
        for h in range(H):
            dst = o_sb[:, 256 * h:256 * h + 256].rearrange("s (e p) -> s e p", e=2)
            src = o_ps[h][:, 0:256].rearrange("s (p e) -> s e p", e=2)
            if h % 2 == 0:
                nc.vector.tensor_scalar(out=dst, in0=src, scalar1=rinv[:, h:h + 1], scalar2=None, op0=ALU.mult)
            else:
                nc.scalar.activation(out=dst, in_=src, func=ACT.Copy, scale=rinv[:, h:h + 1])
        ot_ps = bank_a([P, 1024], BF16, "ot_ps")
        for b8 in range(8):
            nc.tensor.transpose(ot_ps[:, 128 * b8:128 * b8 + 128], o_sb[:, 128 * b8:128 * b8 + 128], ident_b[:])
        ogrp = s_pool.tile([P, 1024], BF16, name="ogrp", tag="s", align_bytes=64)
        for g in range(2):
            copy_on(
                nc,
                "s" if g == 0 else "v",
                ogrp[:, 512 * g:512 * g + 512].rearrange("p (s t) -> p s t", t=4),
                ot_ps[:, 512 * g:512 * g + 512].rearrange("p (t s) -> p s t", t=4),
            )
        oc = s_pool.tile([P, 256], U32, name="oc", tag="s", align_bytes=64)
        osc = s_pool.tile([P, 256], U8, name="osc", tag="s", align_bytes=64)
        nc.vector.quantize_mx(out=oc[:].bitcast(FP8X4), scales=osc[:], in_=ogrp[:])
        for b in range(2):
            y_ps = bank_a([P, 512], F32, "y_ps")
            for i4 in range(4):
                i = 4 * b + i4
                for g in range(2):
                    nc.tensor.matmul_mx(
                        out=y_ps[:, 128 * i4:128 * i4 + 128],
                        lhsT=vcs["w%d" % g][:, 128 * i:128 * i + 128].bitcast(FP8X4),
                        lhsT_scale=vss["w%d" % g][:, 128 * i:128 * i + 128],
                        rhs=oc[:, 128 * g:128 * g + 128].bitcast(FP8X4),
                        rhs_scale=osc[:, 128 * g:128 * g + 128],
                        start=(g == 0),
                        stop=(g == 1),
                    )
            nc.vector.tensor_reduce(
                out=ysum[:, 4 * b:4 * b + 4], in_=y_ps[:].rearrange("p (i s) -> p i s", i=4), axis=AX.X, op=ALU.add
            )
        nc.vector.scalar_tensor_tensor(
            out=res[:], in0=ysum[:], scalar=1.0 / 128.0, in1=b32[:], op0=ALU.mult, op1=ALU.add
        )
        nc.sync.dma_start(out=out.rearrange("(p i) -> p i", i=8), in_=res[:])
